import numpy as np
import ml_dtypes

BF16 = ml_dtypes.bfloat16


def bf(x):
    return np.asarray(x, np.float32).astype(BF16)


def f32(x):
    return np.asarray(x, np.float32)


def f64(x):
    return np.asarray(x).astype(np.float64)


def striped(idx):
    return np.tile(idx.reshape(-1, 16).T, (8, 1))


C, F, S, N = 512, 2048, 1024, 256
EPS = 1e-5


def gelu_tanh(v):
    return 0.5 * v * (1.0 + np.tanh(np.sqrt(2.0 / np.pi) * (v + 0.044715 * v**3)))


def setup_inputs():
    return {
        "base": f32(np.random.standard_normal((C, S))),
        "x": f32(np.random.standard_normal((C, N))),
        "ln_w": f32(1.0 + 0.1 * np.random.standard_normal((C, 1))),
        "ln_b": f32(0.1 * np.random.standard_normal((C, 1))),
        "fc_w": bf(np.random.standard_normal((C, F)) / np.sqrt(C)),
        "fc_b": f32(0.1 * np.random.standard_normal((F, 1))),
        "fc2_w": bf(np.random.standard_normal((F, C)) / np.sqrt(F)),
        "fc2_b": f32(0.1 * np.random.standard_normal((C, 1))),
        "offs": striped(np.random.permutation(S)[:N]),
    }


def reference(base, x, ln_w, ln_b, fc_w, fc_b, fc2_w, fc2_b, offs):
    idx = offs[:16].T.reshape(-1)
    xx = f64(x)
    u = xx.mean(axis=0, keepdims=True)
    s = ((xx - u) ** 2).mean(axis=0, keepdims=True)
    h = f64(ln_w) * (xx - u) / np.sqrt(s + EPS) + f64(ln_b)
    hid = gelu_tanh(f64(fc_w).T @ h + f64(fc_b))
    m = f64(fc2_w).T @ hid + f64(fc2_b)
    out = f64(base).copy()
    out[:, idx] = xx + m
    return out

@@ -1,0 +1,95 @@
+import concourse.mybir as mybir
+from concourse.masks import make_identity
+
+F32, BF16, U16 = mybir.dt.float32, mybir.dt.bfloat16, mybir.dt.uint16
+ACT = mybir.ActivationFunctionType
+ALU = mybir.AluOpType
+
+P = 128
+C, F, S, N = 512, 2048, 1024, 256
+CB, FB = C // P, F // P
+EPS = 1e-5
+FLOPS = 2 * 2 * C * F * N
+
+ROW_LN_W, ROW_LN_B, ROW_FC2_B, ROW_FC_B = 0, CB, 2 * CB, 3 * CB
+ROWS = 3 * CB + FB
+
+
+def tile_splitgpt2_kernel(tc, base, x, ln_w, ln_b, fc_w, fc_b, fc2_w, fc2_b, offs, out):
+    nc = tc.nc
+    with (
+        tc.tile_pool(name="held", bufs=1) as held,
+        tc.tile_pool(name="work", bufs=2) as work,
+        tc.psum_pool(name="stat", bufs=1) as stat,
+        tc.psum_pool(name="accs", bufs=4) as accs,
+    ):
+        x_sb = [held.tile([P, N], F32, name=f"x{k}") for k in range(CB)]
+        for k in range(CB):
+            nc.sync.dma_start(x_sb[k][:], x[k * P : (k + 1) * P, :])
+        offsets = held.tile([P, N // 16], U16, name="offsets")
+        nc.sync.dma_start(offsets[:], offs)
+
+        rows = held.tile([P, P], F32, name="rows")
+        nc.vector.memset(rows[:], 0.0)
+        for vec, row, blocks in ((ln_w, ROW_LN_W, CB), (ln_b, ROW_LN_B, CB), (fc2_b, ROW_FC2_B, CB), (fc_b, ROW_FC_B, FB)):
+            nc.scalar.dma_start(rows[row : row + blocks, :], vec.rearrange("(b p) o -> b (p o)", p=P))
+
+        fcw_sb = [held.tile([P, F], BF16, name=f"fcw{k}") for k in range(CB)]
+        for k in range(CB):
+            nc.sync.dma_start(fcw_sb[k][:], fc_w[k * P : (k + 1) * P, :])
+        fc2w_sb = held.tile([P, FB, C], BF16, name="fc2w")
+        fc2w_view = fc2_w.rearrange("(fb p) c -> p fb c", p=P)
+        for g in range(0, FB, 4):
+            nc.scalar.dma_start(fc2w_sb[:, g : g + 4, :], fc2w_view[:, g : g + 4, :])
+        window = [held.tile([P, S], F32, name=f"window{k}") for k in range(CB)]
+        for k in range(CB):
+            nc.gpsimd.dma_start(window[k][:], base[k * P : (k + 1) * P, :])
+
+        ident = held.tile([P, P], F32, name="ident")
+        make_identity(nc, ident[:])
+        mean_w = held.tile([P, P], F32, name="mean_w")
+        nc.vector.memset(mean_w[:], 1.0 / C)
+        eps = held.tile([P, 1], F32, name="eps")
+        nc.vector.memset(eps[:], EPS)
+
+        cols_ps = stat.tile([P, P], F32, name="cols_ps")
+        nc.tensor.transpose(cols_ps[:], rows[:], ident[:])
+        cols = held.tile([P, ROWS], F32, name="cols")
+        nc.vector.tensor_copy(cols[:], cols_ps[:, :ROWS])
+
+        mean_ps = stat.tile([P, N], F32, name="mean_ps")
+        for k in range(CB):
+            nc.tensor.matmul(mean_ps[:], mean_w[:], x_sb[k][:], start=(k == 0), stop=(k == CB - 1))
+        xc = [held.tile([P, N], F32, name=f"xc{k}") for k in range(CB)]
+        var_ps = stat.tile([P, N], F32, name="var_ps")
+        for k in range(CB):
+            nc.vector.tensor_tensor(xc[k][:], x_sb[k][:], mean_ps[:], ALU.subtract)
+            sq = work.tile([P, N], F32, name="sq")
+            nc.scalar.activation(sq[:], xc[k][:], ACT.Square)
+            nc.tensor.matmul(var_ps[:], mean_w[:], sq[:], start=(k == 0), stop=(k == CB - 1))
+        rstd = held.tile([P, N], F32, name="rstd")
+        nc.scalar.activation(rstd[:], var_ps[:], ACT.Abs_reciprocal_sqrt, bias=eps[:])
+        h = [held.tile([P, N], BF16, name=f"h{k}") for k in range(CB)]
+        for k in range(CB):
+            normed = work.tile([P, N], F32, name="normed")
+            nc.vector.tensor_tensor(normed[:], xc[k][:], rstd[:], ALU.mult)
+            nc.vector.tensor_scalar(
+                h[k][:], normed[:], cols[:, ROW_LN_W + k : ROW_LN_W + k + 1], cols[:, ROW_LN_B + k : ROW_LN_B + k + 1],
+                ALU.mult, ALU.add,
+            )
+
+        hid = [held.tile([P, N], BF16, name=f"hid{f}") for f in range(FB)]
+        for f in range(FB):
+            acc = accs.tile([P, N], F32, name="acc")
+            for k in range(CB):
+                nc.tensor.matmul(acc[:], fcw_sb[k][:, f * P : (f + 1) * P], h[k][:], start=(k == 0), stop=(k == CB - 1))
+            nc.scalar.activation(hid[f][:], acc[:], ACT.Gelu_apprx_tanh, bias=cols[:, ROW_FC_B + f : ROW_FC_B + f + 1])
+
+        for k in range(CB):
+            acc = accs.tile([P, N], F32, name="acc")
+            for f in range(FB):
+                nc.tensor.matmul(acc[:], fc2w_sb[:, f, k * P : (k + 1) * P], hid[f][:], start=(f == 0), stop=(f == FB - 1))
+            m = work.tile([P, N], F32, name="m")
+            nc.scalar.activation(m[:], acc[:], ACT.Identity, bias=cols[:, ROW_FC2_B + k : ROW_FC2_B + k + 1])
+            nc.vector.tensor_tensor(window[k][:].indirect(offsets[:]), x_sb[k][:], m[:], ALU.add)
+            nc.sync.dma_start(out[k * P : (k + 1) * P, :], window[k][:])

@@ -14,6 +14,8 @@ FLOPS = 2 * 2 * C * F * N
 ROW_LN_W, ROW_LN_B, ROW_FC2_B, ROW_FC_B = 0, CB, 2 * CB, 3 * CB
 ROWS = 3 * CB + FB
 
+SIDE_BY_SIDE = 4
+
 
 def tile_splitgpt2_kernel(tc, base, x, ln_w, ln_b, fc_w, fc_b, fc2_w, fc2_b, offs, out):
     nc = tc.nc
@@ -21,16 +23,15 @@ def tile_splitgpt2_kernel(tc, base, x, ln_w, ln_b, fc_w, fc_b, fc2_w, fc2_b, off
         tc.tile_pool(name="held", bufs=1) as held,
         tc.tile_pool(name="work", bufs=2) as work,
         tc.psum_pool(name="stat", bufs=1) as stat,
-        tc.psum_pool(name="accs", bufs=4) as accs,
+        tc.psum_pool(name="accs", bufs=SIDE_BY_SIDE + 1) as accs,
     ):
         x_sb = [held.tile([P, N], F32, name=f"x{k}") for k in range(CB)]
         for k in range(CB):
-            nc.sync.dma_start(x_sb[k][:], x[k * P : (k + 1) * P, :])
-        offsets = held.tile([P, N // 16], U16, name="offsets")
-        nc.sync.dma_start(offsets[:], offs)
+            queue = nc.sync if k < CB // 2 else nc.scalar
+            queue.dma_start(x_sb[k][:], x[k * P : (k + 1) * P, :])
 
         rows = held.tile([P, P], F32, name="rows")
-        nc.vector.memset(rows[:], 0.0)
+        nc.gpsimd.memset(rows[:], 0.0)
         for vec, row, blocks in ((ln_w, ROW_LN_W, CB), (ln_b, ROW_LN_B, CB), (fc2_b, ROW_FC2_B, CB), (fc_b, ROW_FC_B, FB)):
             nc.scalar.dma_start(rows[row : row + blocks, :], vec.rearrange("(b p) o -> b (p o)", p=P))
 
@@ -40,33 +41,42 @@ def tile_splitgpt2_kernel(tc, base, x, ln_w, ln_b, fc_w, fc_b, fc2_w, fc2_b, off
         fc2w_sb = held.tile([P, FB, C], BF16, name="fc2w")
         fc2w_view = fc2_w.rearrange("(fb p) c -> p fb c", p=P)
         for g in range(0, FB, 4):
-            nc.scalar.dma_start(fc2w_sb[:, g : g + 4, :], fc2w_view[:, g : g + 4, :])
+            nc.sync.dma_start(fc2w_sb[:, g : g + 4, :], fc2w_view[:, g : g + 4, :])
+        offsets = held.tile([P, N // 16], U16, name="offsets")
+        nc.sync.dma_start(offsets[:], offs)
         window = [held.tile([P, S], F32, name=f"window{k}") for k in range(CB)]
         for k in range(CB):
-            nc.gpsimd.dma_start(window[k][:], base[k * P : (k + 1) * P, :])
+            nc.sync.dma_start(window[k][:], base[k * P : (k + 1) * P, :])
 
-        ident = held.tile([P, P], F32, name="ident")
-        make_identity(nc, ident[:])
         mean_w = held.tile([P, P], F32, name="mean_w")
         nc.vector.memset(mean_w[:], 1.0 / C)
         eps = held.tile([P, 1], F32, name="eps")
         nc.vector.memset(eps[:], EPS)
+        ident = held.tile([P, P], F32, name="ident")
+        make_identity(nc, ident[:])
+
+        x_sum = held.tile([P, N], F32, name="x_sum")
+        x_sum_hi = held.tile([P, N], F32, name="x_sum_hi")
+        nc.vector.tensor_tensor(x_sum[:], x_sb[0][:], x_sb[1][:], ALU.add)
+        nc.vector.tensor_tensor(x_sum_hi[:], x_sb[2][:], x_sb[3][:], ALU.add)
+        nc.vector.tensor_tensor(x_sum[:], x_sum[:], x_sum_hi[:], ALU.add)
+        mean_ps = stat.tile([P, N], F32, name="mean_ps")
+        nc.tensor.matmul(mean_ps[:], mean_w[:], x_sum[:], start=True, stop=True)
 
         cols_ps = stat.tile([P, P], F32, name="cols_ps")
         nc.tensor.transpose(cols_ps[:], rows[:], ident[:])
-        cols = held.tile([P, ROWS], F32, name="cols")
-        nc.vector.tensor_copy(cols[:], cols_ps[:, :ROWS])
 
-        mean_ps = stat.tile([P, N], F32, name="mean_ps")
-        for k in range(CB):
-            nc.tensor.matmul(mean_ps[:], mean_w[:], x_sb[k][:], start=(k == 0), stop=(k == CB - 1))
         xc = [held.tile([P, N], F32, name=f"xc{k}") for k in range(CB)]
         var_ps = stat.tile([P, N], F32, name="var_ps")
         for k in range(CB):
             nc.vector.tensor_tensor(xc[k][:], x_sb[k][:], mean_ps[:], ALU.subtract)
             sq = work.tile([P, N], F32, name="sq")
-            nc.scalar.activation(sq[:], xc[k][:], ACT.Square)
+            nc.vector.tensor_tensor(sq[:], xc[k][:], xc[k][:], ALU.mult)
             nc.tensor.matmul(var_ps[:], mean_w[:], sq[:], start=(k == 0), stop=(k == CB - 1))
+
+        cols = held.tile([P, ROWS], F32, name="cols")
+        nc.vector.tensor_copy(cols[:], cols_ps[:, :ROWS])
+
         rstd = held.tile([P, N], F32, name="rstd")
         nc.scalar.activation(rstd[:], var_ps[:], ACT.Abs_reciprocal_sqrt, bias=eps[:])
         h = [held.tile([P, N], BF16, name=f"h{k}") for k in range(CB)]
@@ -79,11 +89,24 @@ def tile_splitgpt2_kernel(tc, base, x, ln_w, ln_b, fc_w, fc_b, fc2_w, fc2_b, off
             )
 
         hid = [held.tile([P, N], BF16, name=f"hid{f}") for f in range(FB)]
-        for f in range(FB):
+
+        def fc_matmul(acc, f, k):
+            nc.tensor.matmul(acc[:], fcw_sb[k][:, f * P : (f + 1) * P], h[k][:], start=(k == 0), stop=(k == CB - 1))
+
+        def gelu(acc, f):
+            nc.scalar.activation(hid[f][:], acc[:], ACT.Gelu_apprx_tanh, bias=cols[:, ROW_FC_B + f : ROW_FC_B + f + 1])
+
+        first = [accs.tile([P, N], F32, name="acc") for f in range(SIDE_BY_SIDE)]
+        for k in range(CB):
+            for f in range(SIDE_BY_SIDE):
+                fc_matmul(first[f], f, k)
+        for f in range(SIDE_BY_SIDE):
+            gelu(first[f], f)
+        for f in range(SIDE_BY_SIDE, FB):
             acc = accs.tile([P, N], F32, name="acc")
             for k in range(CB):
-                nc.tensor.matmul(acc[:], fcw_sb[k][:, f * P : (f + 1) * P], h[k][:], start=(k == 0), stop=(k == CB - 1))
-            nc.scalar.activation(hid[f][:], acc[:], ACT.Gelu_apprx_tanh, bias=cols[:, ROW_FC_B + f : ROW_FC_B + f + 1])
+                fc_matmul(acc, f, k)
+            gelu(acc, f)
 
         for k in range(CB):
             acc = accs.tile([P, N], F32, name="acc")

@@ -25,10 +25,11 @@ def tile_splitgpt2_kernel(tc, base, x, ln_w, ln_b, fc_w, fc_b, fc2_w, fc2_b, off
         tc.psum_pool(name="stat", bufs=1) as stat,
         tc.psum_pool(name="accs", bufs=SIDE_BY_SIDE + 1) as accs,
     ):
-        x_sb = [held.tile([P, N], F32, name=f"x{k}") for k in range(CB)]
-        for k in range(CB):
-            queue = nc.sync if k < CB // 2 else nc.scalar
-            queue.dma_start(x_sb[k][:], x[k * P : (k + 1) * P, :])
+        x_all = held.tile([P, CB, N], F32, name="x_all")
+        x_view = x.rearrange("(k p) n -> p k n", p=P)
+        nc.sync.dma_start(x_all[:, : CB // 2, :], x_view[:, : CB // 2, :])
+        nc.scalar.dma_start(x_all[:, CB // 2 :, :], x_view[:, CB // 2 :, :])
+        x_sb = [x_all[:, k, :] for k in range(CB)]
 
         rows = held.tile([P, P], F32, name="rows")
         nc.gpsimd.memset(rows[:], 0.0)
@@ -55,25 +56,23 @@ def tile_splitgpt2_kernel(tc, base, x, ln_w, ln_b, fc_w, fc_b, fc2_w, fc2_b, off
         ident = held.tile([P, P], F32, name="ident")
         make_identity(nc, ident[:])
 
+        x_pairs = held.tile([P, CB // 2, N], F32, name="x_pairs")
+        nc.vector.tensor_tensor(x_pairs[:], x_all[:, : CB // 2, :], x_all[:, CB // 2 :, :], ALU.add)
         x_sum = held.tile([P, N], F32, name="x_sum")
-        x_sum_hi = held.tile([P, N], F32, name="x_sum_hi")
-        nc.vector.tensor_tensor(x_sum[:], x_sb[0][:], x_sb[1][:], ALU.add)
-        nc.vector.tensor_tensor(x_sum_hi[:], x_sb[2][:], x_sb[3][:], ALU.add)
-        nc.vector.tensor_tensor(x_sum[:], x_sum[:], x_sum_hi[:], ALU.add)
+        nc.vector.tensor_tensor(x_sum[:], x_pairs[:, 0, :], x_pairs[:, 1, :], ALU.add)
         mean_ps = stat.tile([P, N], F32, name="mean_ps")
         nc.tensor.matmul(mean_ps[:], mean_w[:], x_sum[:], start=True, stop=True)
-
-        cols_ps = stat.tile([P, P], F32, name="cols_ps")
-        nc.tensor.transpose(cols_ps[:], rows[:], ident[:])
 
         xc = [held.tile([P, N], F32, name=f"xc{k}") for k in range(CB)]
         var_ps = stat.tile([P, N], F32, name="var_ps")
         for k in range(CB):
-            nc.vector.tensor_tensor(xc[k][:], x_sb[k][:], mean_ps[:], ALU.subtract)
+            nc.vector.tensor_tensor(xc[k][:], x_sb[k], mean_ps[:], ALU.subtract)
             sq = work.tile([P, N], F32, name="sq")
             nc.vector.tensor_tensor(sq[:], xc[k][:], xc[k][:], ALU.mult)
             nc.tensor.matmul(var_ps[:], mean_w[:], sq[:], start=(k == 0), stop=(k == CB - 1))
 
+        cols_ps = stat.tile([P, P], F32, name="cols_ps")
+        nc.tensor.transpose(cols_ps[:], rows[:], ident[:])
         cols = held.tile([P, ROWS], F32, name="cols")
         nc.vector.tensor_copy(cols[:], cols_ps[:, :ROWS])
 
@@ -114,5 +113,5 @@ def tile_splitgpt2_kernel(tc, base, x, ln_w, ln_b, fc_w, fc_b, fc2_w, fc2_b, off
                 nc.tensor.matmul(acc[:], fc2w_sb[:, f, k * P : (k + 1) * P], hid[f][:], start=(f == 0), stop=(f == FB - 1))
             m = work.tile([P, N], F32, name="m")
             nc.scalar.activation(m[:], acc[:], ACT.Identity, bias=cols[:, ROW_FC2_B + k : ROW_FC2_B + k + 1])
-            nc.vector.tensor_tensor(window[k][:].indirect(offsets[:]), x_sb[k][:], m[:], ALU.add)
+            nc.vector.tensor_tensor(window[k][:].indirect(offsets[:]), x_sb[k], m[:], ALU.add)
             nc.sync.dma_start(out[k * P : (k + 1) * P, :], window[k][:])

@@ -16,6 +16,9 @@ ROWS = 3 * CB + FB
 
 SIDE_BY_SIDE = 4
 
+WARM_UP = 5
+KEEP_WARM = 2
+
 
 def tile_splitgpt2_kernel(tc, base, x, ln_w, ln_b, fc_w, fc_b, fc2_w, fc2_b, offs, out):
     nc = tc.nc
@@ -56,11 +59,18 @@ def tile_splitgpt2_kernel(tc, base, x, ln_w, ln_b, fc_w, fc_b, fc2_w, fc2_b, off
         ident = held.tile([P, P], F32, name="ident")
         make_identity(nc, ident[:])
 
+        mean_ps = stat.tile([P, N], F32, name="mean_ps")
+
+        def idle_matmuls(count):
+            for i in range(count):
+                nc.tensor.matmul(mean_ps[:, :P], mean_w[:], mean_w[:], start=True, stop=True)
+
+        idle_matmuls(WARM_UP)
+
         x_pairs = held.tile([P, CB // 2, N], F32, name="x_pairs")
         nc.vector.tensor_tensor(x_pairs[:], x_all[:, : CB // 2, :], x_all[:, CB // 2 :, :], ALU.add)
         x_sum = held.tile([P, N], F32, name="x_sum")
         nc.vector.tensor_tensor(x_sum[:], x_pairs[:, 0, :], x_pairs[:, 1, :], ALU.add)
-        mean_ps = stat.tile([P, N], F32, name="mean_ps")
         nc.tensor.matmul(mean_ps[:], mean_w[:], x_sum[:], start=True, stop=True)
 
         xc = [held.tile([P, N], F32, name=f"xc{k}") for k in range(CB)]
@@ -73,6 +83,7 @@ def tile_splitgpt2_kernel(tc, base, x, ln_w, ln_b, fc_w, fc_b, fc2_w, fc2_b, off
 
         cols_ps = stat.tile([P, P], F32, name="cols_ps")
         nc.tensor.transpose(cols_ps[:], rows[:], ident[:])
+        idle_matmuls(KEEP_WARM)
         cols = held.tile([P, ROWS], F32, name="cols")
         nc.vector.tensor_copy(cols[:], cols_ps[:, :ROWS])
 

@@ -7,7 +7,7 @@ ALU = mybir.AluOpType
 
 P = 128
 C, F, S, N = 512, 2048, 1024, 256
-CB, FB = C // P, F // P
+CB, FB, TB = C // P, F // P, N // P
 EPS = 1e-5
 FLOPS = 2 * 2 * C * F * N
 
@@ -16,8 +16,9 @@ ROWS = 3 * CB + FB
 
 SIDE_BY_SIDE = 4
 
-WARM_UP = 5
-KEEP_WARM = 2
+IDLE_UNTIL_X = 4
+IDLE_UNTIL_NORMED = 7
+IDLE_UNTIL_H = 2
 
 
 def tile_splitgpt2_kernel(tc, base, x, ln_w, ln_b, fc_w, fc_b, fc2_w, fc2_b, offs, out):
@@ -25,14 +26,12 @@ def tile_splitgpt2_kernel(tc, base, x, ln_w, ln_b, fc_w, fc_b, fc2_w, fc2_b, off
     with (
         tc.tile_pool(name="held", bufs=1) as held,
         tc.tile_pool(name="work", bufs=2) as work,
-        tc.psum_pool(name="stat", bufs=1) as stat,
-        tc.psum_pool(name="accs", bufs=SIDE_BY_SIDE + 1) as accs,
+        tc.psum_pool(name="banks", bufs=8) as banks,
     ):
         x_all = held.tile([P, CB, N], F32, name="x_all")
         x_view = x.rearrange("(k p) n -> p k n", p=P)
-        nc.sync.dma_start(x_all[:, : CB // 2, :], x_view[:, : CB // 2, :])
-        nc.scalar.dma_start(x_all[:, CB // 2 :, :], x_view[:, CB // 2 :, :])
-        x_sb = [x_all[:, k, :] for k in range(CB)]
+        for t in range(TB):
+            nc.sync.dma_start(x_all[:, :, t * P : (t + 1) * P], x_view[:, :, t * P : (t + 1) * P])
 
         rows = held.tile([P, P], F32, name="rows")
         nc.gpsimd.memset(rows[:], 0.0)
@@ -52,51 +51,57 @@ def tile_splitgpt2_kernel(tc, base, x, ln_w, ln_b, fc_w, fc_b, fc2_w, fc2_b, off
         for k in range(CB):
             nc.sync.dma_start(window[k][:], base[k * P : (k + 1) * P, :])
 
-        mean_w = held.tile([P, P], F32, name="mean_w")
-        nc.vector.memset(mean_w[:], 1.0 / C)
-        eps = held.tile([P, 1], F32, name="eps")
-        nc.vector.memset(eps[:], EPS)
+        idle_in = held.tile([P, P], F32, name="idle_in")
+        nc.vector.memset(idle_in[:], 1.0)
         ident = held.tile([P, P], F32, name="ident")
         make_identity(nc, ident[:])
+        eps = held.tile([P, 1], F32, name="eps")
+        nc.vector.memset(eps[:], EPS)
 
-        mean_ps = stat.tile([P, N], F32, name="mean_ps")
+        def bank(columns):
+            return banks.tile([P, columns], F32, name="bank")
+
+        idle_ps = bank(P)
 
         def idle_matmuls(count):
             for i in range(count):
-                nc.tensor.matmul(mean_ps[:, :P], mean_w[:], mean_w[:], start=True, stop=True)
+                nc.tensor.matmul(idle_ps[:], idle_in[:], idle_in[:], start=True, stop=True)
 
-        idle_matmuls(WARM_UP)
+        idle_matmuls(IDLE_UNTIL_X)
 
-        x_pairs = held.tile([P, CB // 2, N], F32, name="x_pairs")
-        nc.vector.tensor_tensor(x_pairs[:], x_all[:, : CB // 2, :], x_all[:, CB // 2 :, :], ALU.add)
-        x_sum = held.tile([P, N], F32, name="x_sum")
-        nc.vector.tensor_tensor(x_sum[:], x_pairs[:, 0, :], x_pairs[:, 1, :], ALU.add)
-        nc.tensor.matmul(mean_ps[:], mean_w[:], x_sum[:], start=True, stop=True)
-
-        xc = [held.tile([P, N], F32, name=f"xc{k}") for k in range(CB)]
-        var_ps = stat.tile([P, N], F32, name="var_ps")
-        for k in range(CB):
-            nc.vector.tensor_tensor(xc[k][:], x_sb[k], mean_ps[:], ALU.subtract)
-            sq = work.tile([P, N], F32, name="sq")
-            nc.vector.tensor_tensor(sq[:], xc[k][:], xc[k][:], ALU.mult)
-            nc.tensor.matmul(var_ps[:], mean_w[:], sq[:], start=(k == 0), stop=(k == CB - 1))
-
-        cols_ps = stat.tile([P, P], F32, name="cols_ps")
+        x_t = [bank(C) for t in range(TB)]
+        for t in range(TB):
+            for k in range(CB):
+                nc.tensor.transpose(x_t[t][:, k * P : (k + 1) * P], x_all[:, k, t * P : (t + 1) * P], ident[:])
+        cols_ps = bank(P)
         nc.tensor.transpose(cols_ps[:], rows[:], ident[:])
-        idle_matmuls(KEEP_WARM)
+        idle_matmuls(IDLE_UNTIL_NORMED)
+
+        mean_var = [held.tile([P, 2], F32, name=f"mean_var{t}") for t in range(TB)]
+        rstd = [held.tile([P, 1], F32, name=f"rstd{t}") for t in range(TB)]
+        for t in range(TB):
+            stats = work.tile([P, 6], F32, name="stats")
+            nc.vector.bn_stats(stats[:], x_t[t][:])
+            nc.vector.bn_aggr(mean_var[t][:], stats[:])
+            nc.scalar.activation(rstd[t][:], mean_var[t][:, 1:2], ACT.Abs_reciprocal_sqrt, bias=eps[:])
+        normed = [held.tile([P, C], F32, name=f"normed{t}") for t in range(TB)]
+        normed_t = [bank(N) for k in range(CB)]
+        for first_k in range(0, CB, CB // 2):
+            half = slice(first_k * P, (first_k + CB // 2) * P)
+            for t in range(TB):
+                nc.vector.tensor_scalar(
+                    normed[t][:, half], x_t[t][:, half], mean_var[t][:, 0:1], rstd[t][:], ALU.subtract, ALU.mult
+                )
+                for k in range(first_k, first_k + CB // 2):
+                    nc.tensor.transpose(normed_t[k][:, t * P : (t + 1) * P], normed[t][:, k * P : (k + 1) * P], ident[:])
+        idle_matmuls(IDLE_UNTIL_H)
         cols = held.tile([P, ROWS], F32, name="cols")
         nc.vector.tensor_copy(cols[:], cols_ps[:, :ROWS])
 
-        rstd = held.tile([P, N], F32, name="rstd")
-        nc.scalar.activation(rstd[:], var_ps[:], ACT.Abs_reciprocal_sqrt, bias=eps[:])
         h = [held.tile([P, N], BF16, name=f"h{k}") for k in range(CB)]
         for k in range(CB):
-            normed = work.tile([P, N], F32, name="normed")
-            nc.vector.tensor_tensor(normed[:], xc[k][:], rstd[:], ALU.mult)
-            nc.vector.tensor_scalar(
-                h[k][:], normed[:], cols[:, ROW_LN_W + k : ROW_LN_W + k + 1], cols[:, ROW_LN_B + k : ROW_LN_B + k + 1],
-                ALU.mult, ALU.add,
-            )
+            gain, bias = cols[:, ROW_LN_W + k : ROW_LN_W + k + 1], cols[:, ROW_LN_B + k : ROW_LN_B + k + 1]
+            nc.vector.tensor_scalar(h[k][:], normed_t[k][:], gain, bias, ALU.mult, ALU.add)
 
         hid = [held.tile([P, N], BF16, name=f"hid{f}") for f in range(FB)]
 
@@ -106,23 +111,23 @@ def tile_splitgpt2_kernel(tc, base, x, ln_w, ln_b, fc_w, fc_b, fc2_w, fc2_b, off
         def gelu(acc, f):
             nc.scalar.activation(hid[f][:], acc[:], ACT.Gelu_apprx_tanh, bias=cols[:, ROW_FC_B + f : ROW_FC_B + f + 1])
 
-        first = [accs.tile([P, N], F32, name="acc") for f in range(SIDE_BY_SIDE)]
+        first = [bank(N) for f in range(SIDE_BY_SIDE)]
         for k in range(CB):
             for f in range(SIDE_BY_SIDE):
                 fc_matmul(first[f], f, k)
         for f in range(SIDE_BY_SIDE):
             gelu(first[f], f)
         for f in range(SIDE_BY_SIDE, FB):
-            acc = accs.tile([P, N], F32, name="acc")
+            acc = bank(N)
             for k in range(CB):
                 fc_matmul(acc, f, k)
             gelu(acc, f)
 
         for k in range(CB):
-            acc = accs.tile([P, N], F32, name="acc")
+            acc = bank(N)
             for f in range(FB):
                 nc.tensor.matmul(acc[:], fc2w_sb[:, f, k * P : (k + 1) * P], hid[f][:], start=(f == 0), stop=(f == FB - 1))
             m = work.tile([P, N], F32, name="m")
             nc.scalar.activation(m[:], acc[:], ACT.Identity, bias=cols[:, ROW_FC2_B + k : ROW_FC2_B + k + 1])
-            nc.vector.tensor_tensor(window[k][:].indirect(offsets[:]), x_sb[k], m[:], ALU.add)
+            nc.vector.tensor_tensor(window[k][:].indirect(offsets[:]), x_all[:, k, :], m[:], ALU.add)
             nc.sync.dma_start(out[k * P : (k + 1) * P, :], window[k][:])

@@ -17,8 +17,9 @@ ROWS = 3 * CB + FB
 SIDE_BY_SIDE = 4
 
 IDLE_UNTIL_X = 4
-IDLE_UNTIL_NORMED = 7
-IDLE_UNTIL_H = 2
+IDLE_UNTIL_X_REST = 2
+IDLE_UNTIL_NORMED = 6
+IDLE_UNTIL_NEXT_PIECE = 1
 
 
 def tile_splitgpt2_kernel(tc, base, x, ln_w, ln_b, fc_w, fc_b, fc2_w, fc2_b, offs, out):
@@ -63,19 +64,21 @@ def tile_splitgpt2_kernel(tc, base, x, ln_w, ln_b, fc_w, fc_b, fc2_w, fc2_b, off
 
         idle_ps = bank(P)
 
-        def idle_matmuls(count):
+        def idle_matmuls(count, moving):
             for i in range(count):
-                nc.tensor.matmul(idle_ps[:], idle_in[:], idle_in[:], start=True, stop=True)
+                nc.tensor.matmul(idle_ps[:], idle_in[:], moving, start=True, stop=True)
 
-        idle_matmuls(IDLE_UNTIL_X)
+        idle_matmuls(IDLE_UNTIL_X, idle_in[:])
 
         x_t = [bank(C) for t in range(TB)]
+        cols_ps = bank(P)
         for t in range(TB):
             for k in range(CB):
                 nc.tensor.transpose(x_t[t][:, k * P : (k + 1) * P], x_all[:, k, t * P : (t + 1) * P], ident[:])
-        cols_ps = bank(P)
+            if t < TB - 1:
+                idle_matmuls(IDLE_UNTIL_X_REST, x_all[:, CB - 1, t * P : (t + 1) * P])
         nc.tensor.transpose(cols_ps[:], rows[:], ident[:])
-        idle_matmuls(IDLE_UNTIL_NORMED)
+        idle_matmuls(IDLE_UNTIL_NORMED, x_all[:, CB - 1, N - P :])
 
         mean_var = [held.tile([P, 2], F32, name=f"mean_var{t}") for t in range(TB)]
         rstd = [held.tile([P, 1], F32, name=f"rstd{t}") for t in range(TB)]
@@ -94,7 +97,7 @@ def tile_splitgpt2_kernel(tc, base, x, ln_w, ln_b, fc_w, fc_b, fc2_w, fc2_b, off
                 )
                 for k in range(first_k, first_k + CB // 2):
                     nc.tensor.transpose(normed_t[k][:, t * P : (t + 1) * P], normed[t][:, k * P : (k + 1) * P], ident[:])
-        idle_matmuls(IDLE_UNTIL_H)
+                idle_matmuls(IDLE_UNTIL_NEXT_PIECE, normed[t][:, first_k * P : (first_k + 1) * P])
         cols = held.tile([P, ROWS], F32, name="cols")
         nc.vector.tensor_copy(cols[:], cols_ps[:, :ROWS])
 

@@ -16,10 +16,7 @@ ROWS = 3 * CB + FB
 
 SIDE_BY_SIDE = 4
 
-IDLE_UNTIL_X = 4
-IDLE_UNTIL_X_REST = 2
-IDLE_UNTIL_NORMED = 6
-IDLE_UNTIL_NEXT_PIECE = 1
+FC_GROUP = 4
 
 
 def tile_splitgpt2_kernel(tc, base, x, ln_w, ln_b, fc_w, fc_b, fc2_w, fc2_b, offs, out):
@@ -37,11 +34,15 @@ def tile_splitgpt2_kernel(tc, base, x, ln_w, ln_b, fc_w, fc_b, fc2_w, fc2_b, off
         rows = held.tile([P, P], F32, name="rows")
         nc.gpsimd.memset(rows[:], 0.0)
         for vec, row, blocks in ((ln_w, ROW_LN_W, CB), (ln_b, ROW_LN_B, CB), (fc2_b, ROW_FC2_B, CB), (fc_b, ROW_FC_B, FB)):
-            nc.scalar.dma_start(rows[row : row + blocks, :], vec.rearrange("(b p) o -> b (p o)", p=P))
+            nc.sync.dma_start(rows[row : row + blocks, :], vec.rearrange("(b p) o -> b (p o)", p=P))
 
-        fcw_sb = [held.tile([P, F], BF16, name=f"fcw{k}") for k in range(CB)]
-        for k in range(CB):
-            nc.sync.dma_start(fcw_sb[k][:], fc_w[k * P : (k + 1) * P, :])
+        fcw_sb = [held.tile([P, CB, FC_GROUP * P], BF16, name=f"fcw{g}") for g in range(FB // FC_GROUP)]
+        fcw_view = fc_w.rearrange("(k p) f -> p k f", p=P)
+        for g in range(FB // FC_GROUP):
+            nc.sync.dma_start(fcw_sb[g][:], fcw_view[:, :, g * FC_GROUP * P : (g + 1) * FC_GROUP * P])
+
+        def fcw_block(f, k):
+            return fcw_sb[f // FC_GROUP][:, k, (f % FC_GROUP) * P : (f % FC_GROUP + 1) * P]
         fc2w_sb = held.tile([P, FB, C], BF16, name="fc2w")
         fc2w_view = fc2_w.rearrange("(fb p) c -> p fb c", p=P)
         for g in range(0, FB, 4):
@@ -52,33 +53,20 @@ def tile_splitgpt2_kernel(tc, base, x, ln_w, ln_b, fc_w, fc_b, fc2_w, fc2_b, off
         for k in range(CB):
             nc.sync.dma_start(window[k][:], base[k * P : (k + 1) * P, :])
 
-        idle_in = held.tile([P, P], F32, name="idle_in")
-        nc.vector.memset(idle_in[:], 1.0)
         ident = held.tile([P, P], F32, name="ident")
         make_identity(nc, ident[:])
         eps = held.tile([P, 1], F32, name="eps")
-        nc.vector.memset(eps[:], EPS)
+        nc.gpsimd.memset(eps[:], EPS)
 
         def bank(columns):
             return banks.tile([P, columns], F32, name="bank")
-
-        idle_ps = bank(P)
-
-        def idle_matmuls(count, moving):
-            for i in range(count):
-                nc.tensor.matmul(idle_ps[:], idle_in[:], moving, start=True, stop=True)
-
-        idle_matmuls(IDLE_UNTIL_X, idle_in[:])
 
         x_t = [bank(C) for t in range(TB)]
         cols_ps = bank(P)
         for t in range(TB):
             for k in range(CB):
                 nc.tensor.transpose(x_t[t][:, k * P : (k + 1) * P], x_all[:, k, t * P : (t + 1) * P], ident[:])
-            if t < TB - 1:
-                idle_matmuls(IDLE_UNTIL_X_REST, x_all[:, CB - 1, t * P : (t + 1) * P])
         nc.tensor.transpose(cols_ps[:], rows[:], ident[:])
-        idle_matmuls(IDLE_UNTIL_NORMED, x_all[:, CB - 1, N - P :])
 
         mean_var = [held.tile([P, 2], F32, name=f"mean_var{t}") for t in range(TB)]
         rstd = [held.tile([P, 1], F32, name=f"rstd{t}") for t in range(TB)]
@@ -87,37 +75,48 @@ def tile_splitgpt2_kernel(tc, base, x, ln_w, ln_b, fc_w, fc_b, fc2_w, fc2_b, off
             nc.vector.bn_stats(stats[:], x_t[t][:])
             nc.vector.bn_aggr(mean_var[t][:], stats[:])
             nc.scalar.activation(rstd[t][:], mean_var[t][:, 1:2], ACT.Abs_reciprocal_sqrt, bias=eps[:])
+        HALF = CB // 2
         normed = [held.tile([P, C], F32, name=f"normed{t}") for t in range(TB)]
-        normed_t = [bank(N) for k in range(CB)]
-        for first_k in range(0, CB, CB // 2):
-            half = slice(first_k * P, (first_k + CB // 2) * P)
-            for t in range(TB):
+        normed_t = [[bank(HALF * P) for first_k in range(0, CB, HALF)] for t in range(TB)]
+        for t in range(TB):
+            for first_k in range(0, CB, HALF):
+                half = slice(first_k * P, (first_k + HALF) * P)
                 nc.vector.tensor_scalar(
                     normed[t][:, half], x_t[t][:, half], mean_var[t][:, 0:1], rstd[t][:], ALU.subtract, ALU.mult
                 )
-                for k in range(first_k, first_k + CB // 2):
-                    nc.tensor.transpose(normed_t[k][:, t * P : (t + 1) * P], normed[t][:, k * P : (k + 1) * P], ident[:])
-                idle_matmuls(IDLE_UNTIL_NEXT_PIECE, normed[t][:, first_k * P : (first_k + 1) * P])
+                for i in range(HALF):
+                    k = first_k + i
+                    nc.tensor.transpose(
+                        normed_t[t][first_k // HALF][:, i * P : (i + 1) * P], normed[t][:, k * P : (k + 1) * P], ident[:]
+                    )
+
         cols = held.tile([P, ROWS], F32, name="cols")
         nc.vector.tensor_copy(cols[:], cols_ps[:, :ROWS])
 
         h = [held.tile([P, N], BF16, name=f"h{k}") for k in range(CB)]
-        for k in range(CB):
-            gain, bias = cols[:, ROW_LN_W + k : ROW_LN_W + k + 1], cols[:, ROW_LN_B + k : ROW_LN_B + k + 1]
-            nc.vector.tensor_scalar(h[k][:], normed_t[k][:], gain, bias, ALU.mult, ALU.add)
+        for t in range(TB):
+            for k in range(CB):
+                gain, bias = cols[:, ROW_LN_W + k : ROW_LN_W + k + 1], cols[:, ROW_LN_B + k : ROW_LN_B + k + 1]
+                turned = normed_t[t][k // HALF][:, (k % HALF) * P : (k % HALF + 1) * P]
+                if t == 0:
+                    nc.scalar.activation(h[k][:, t * P : (t + 1) * P], turned, ACT.Identity, bias=bias, scale=gain)
+                else:
+                    nc.vector.tensor_scalar(h[k][:, t * P : (t + 1) * P], turned, gain, bias, ALU.mult, ALU.add)
 
         hid = [held.tile([P, N], BF16, name=f"hid{f}") for f in range(FB)]
 
         def fc_matmul(acc, f, k):
-            nc.tensor.matmul(acc[:], fcw_sb[k][:, f * P : (f + 1) * P], h[k][:], start=(k == 0), stop=(k == CB - 1))
+            nc.tensor.matmul(acc[:], fcw_block(f, k), h[k][:], start=(k == 0), stop=(k == CB - 1))
 
         def gelu(acc, f):
             nc.scalar.activation(hid[f][:], acc[:], ACT.Gelu_apprx_tanh, bias=cols[:, ROW_FC_B + f : ROW_FC_B + f + 1])
 
         first = [bank(N) for f in range(SIDE_BY_SIDE)]
-        for k in range(CB):
-            for f in range(SIDE_BY_SIDE):
-                fc_matmul(first[f], f, k)
+        for t in range(TB):
+            tokens = slice(t * P, (t + 1) * P)
+            for k in range(CB):
+                for f in range(SIDE_BY_SIDE):
+                    nc.tensor.matmul(first[f][:, tokens], fcw_block(f, k), h[k][:, tokens], start=(k == 0), stop=(k == CB - 1))
         for f in range(SIDE_BY_SIDE):
             gelu(first[f], f)
         for f in range(SIDE_BY_SIDE, FB):

@@ -18,6 +18,10 @@ SIDE_BY_SIDE = 4
 
 FC_GROUP = 4
 
+IDLE_UNTIL_X = 3
+IDLE_UNTIL_X_REST = 1
+IDLE_UNTIL_NORMED = 3
+
 
 def tile_splitgpt2_kernel(tc, base, x, ln_w, ln_b, fc_w, fc_b, fc2_w, fc2_b, offs, out):
     nc = tc.nc
@@ -53,6 +57,8 @@ def tile_splitgpt2_kernel(tc, base, x, ln_w, ln_b, fc_w, fc_b, fc2_w, fc2_b, off
         for k in range(CB):
             nc.sync.dma_start(window[k][:], base[k * P : (k + 1) * P, :])
 
+        idle_in = held.tile([P, P], F32, name="idle_in")
+        nc.vector.memset(idle_in[:], 1.0)
         ident = held.tile([P, P], F32, name="ident")
         make_identity(nc, ident[:])
         eps = held.tile([P, 1], F32, name="eps")
@@ -61,12 +67,23 @@ def tile_splitgpt2_kernel(tc, base, x, ln_w, ln_b, fc_w, fc_b, fc2_w, fc2_b, off
         def bank(columns):
             return banks.tile([P, columns], F32, name="bank")
 
+        idle_ps = bank(P)
+
+        def idle_matmuls(count, moving):
+            for i in range(count):
+                nc.tensor.matmul(idle_ps[:], idle_in[:], moving, start=True, stop=True)
+
+        idle_matmuls(IDLE_UNTIL_X, idle_in[:])
+
         x_t = [bank(C) for t in range(TB)]
         cols_ps = bank(P)
         for t in range(TB):
             for k in range(CB):
                 nc.tensor.transpose(x_t[t][:, k * P : (k + 1) * P], x_all[:, k, t * P : (t + 1) * P], ident[:])
+            if t < TB - 1:
+                idle_matmuls(IDLE_UNTIL_X_REST, x_all[:, CB - 1, t * P : (t + 1) * P])
         nc.tensor.transpose(cols_ps[:], rows[:], ident[:])
+        idle_matmuls(IDLE_UNTIL_NORMED, x_all[:, CB - 1, N - P :])
 
         mean_var = [held.tile([P, 2], F32, name=f"mean_var{t}") for t in range(TB)]
         rstd = [held.tile([P, 1], F32, name=f"rstd{t}") for t in range(TB)]

@@ -18,8 +18,6 @@ SIDE_BY_SIDE = 4
 
 FC_GROUP = 4
 
-IDLE_UNTIL_X = 3
-IDLE_UNTIL_X_REST = 1
 IDLE_UNTIL_NORMED = 3
 
 
@@ -73,15 +71,11 @@ def tile_splitgpt2_kernel(tc, base, x, ln_w, ln_b, fc_w, fc_b, fc2_w, fc2_b, off
             for i in range(count):
                 nc.tensor.matmul(idle_ps[:], idle_in[:], moving, start=True, stop=True)
 
-        idle_matmuls(IDLE_UNTIL_X, idle_in[:])
-
         x_t = [bank(C) for t in range(TB)]
         cols_ps = bank(P)
         for t in range(TB):
             for k in range(CB):
                 nc.tensor.transpose(x_t[t][:, k * P : (k + 1) * P], x_all[:, k, t * P : (t + 1) * P], ident[:])
-            if t < TB - 1:
-                idle_matmuls(IDLE_UNTIL_X_REST, x_all[:, CB - 1, t * P : (t + 1) * P])
         nc.tensor.transpose(cols_ps[:], rows[:], ident[:])
         idle_matmuls(IDLE_UNTIL_NORMED, x_all[:, CB - 1, N - P :])
 

@@ -71,29 +71,32 @@ def tile_splitgpt2_kernel(tc, base, x, ln_w, ln_b, fc_w, fc_b, fc2_w, fc2_b, off
             for i in range(count):
                 nc.tensor.matmul(idle_ps[:], idle_in[:], moving, start=True, stop=True)
 
-        x_t = [bank(C) for t in range(TB)]
+        HALF = CB // 2
+        x_t = [[bank(HALF * P) for first_k in range(0, CB, HALF)] for t in range(TB)]
         cols_ps = bank(P)
         for t in range(TB):
             for k in range(CB):
-                nc.tensor.transpose(x_t[t][:, k * P : (k + 1) * P], x_all[:, k, t * P : (t + 1) * P], ident[:])
+                nc.tensor.transpose(
+                    x_t[t][k // HALF][:, (k % HALF) * P : (k % HALF + 1) * P], x_all[:, k, t * P : (t + 1) * P], ident[:]
+                )
         nc.tensor.transpose(cols_ps[:], rows[:], ident[:])
         idle_matmuls(IDLE_UNTIL_NORMED, x_all[:, CB - 1, N - P :])
 
         mean_var = [held.tile([P, 2], F32, name=f"mean_var{t}") for t in range(TB)]
         rstd = [held.tile([P, 1], F32, name=f"rstd{t}") for t in range(TB)]
         for t in range(TB):
-            stats = work.tile([P, 6], F32, name="stats")
-            nc.vector.bn_stats(stats[:], x_t[t][:])
+            stats = work.tile([P, 2 * 6], F32, name="stats")
+            for i in range(2):
+                nc.vector.bn_stats(stats[:, i * 6 : (i + 1) * 6], x_t[t][i][:])
             nc.vector.bn_aggr(mean_var[t][:], stats[:])
             nc.scalar.activation(rstd[t][:], mean_var[t][:, 1:2], ACT.Abs_reciprocal_sqrt, bias=eps[:])
-        HALF = CB // 2
         normed = [held.tile([P, C], F32, name=f"normed{t}") for t in range(TB)]
         normed_t = [[bank(HALF * P) for first_k in range(0, CB, HALF)] for t in range(TB)]
         for t in range(TB):
             for first_k in range(0, CB, HALF):
                 half = slice(first_k * P, (first_k + HALF) * P)
                 nc.vector.tensor_scalar(
-                    normed[t][:, half], x_t[t][:, half], mean_var[t][:, 0:1], rstd[t][:], ALU.subtract, ALU.mult
+                    normed[t][:, half], x_t[t][first_k // HALF][:], mean_var[t][:, 0:1], rstd[t][:], ALU.subtract, ALU.mult
                 )
                 for i in range(HALF):
                     k = first_k + i

@@ -31,7 +31,11 @@ def tile_splitgpt2_kernel(tc, base, x, ln_w, ln_b, fc_w, fc_b, fc2_w, fc2_b, off
         x_all = held.tile([P, CB, N], F32, name="x_all")
         x_view = x.rearrange("(k p) n -> p k n", p=P)
         for t in range(TB):
-            nc.sync.dma_start(x_all[:, :, t * P : (t + 1) * P], x_view[:, :, t * P : (t + 1) * P])
+            for first_k in range(0, CB, CB // 2):
+                nc.sync.dma_start(
+                    x_all[:, first_k : first_k + CB // 2, t * P : (t + 1) * P],
+                    x_view[:, first_k : first_k + CB // 2, t * P : (t + 1) * P],
+                )
 
         rows = held.tile([P, P], F32, name="rows")
         nc.gpsimd.memset(rows[:], 0.0)

@@ -31,8 +31,8 @@ def tile_splitgpt2_kernel(tc, base, x, ln_w, ln_b, fc_w, fc_b, fc2_w, fc2_b, off
         x_all = held.tile([P, CB, N], F32, name="x_all")
         x_view = x.rearrange("(k p) n -> p k n", p=P)
         for t in range(TB):
-            for first_k in range(0, CB, CB // 2):
-                nc.sync.dma_start(
+            for queue, first_k in ((nc.sync, 0), (nc.scalar, CB // 2)):
+                queue.dma_start(
                     x_all[:, first_k : first_k + CB // 2, t * P : (t + 1) * P],
                     x_view[:, first_k : first_k + CB // 2, t * P : (t + 1) * P],
                 )

@@ -16,6 +16,8 @@ ROWS = 3 * CB + FB
 
 SIDE_BY_SIDE = 4
 
+LAST_TOKENS = 64
+
 FC_GROUP = 4
 
 IDLE_UNTIL_NORMED = 3
@@ -144,10 +146,13 @@ def tile_splitgpt2_kernel(tc, base, x, ln_w, ln_b, fc_w, fc_b, fc2_w, fc2_b, off
             gelu(acc, f)
 
         for k in range(CB):
-            acc = bank(N)
-            for f in range(FB):
-                nc.tensor.matmul(acc[:], fc2w_sb[:, f, k * P : (k + 1) * P], hid[f][:], start=(f == 0), stop=(f == FB - 1))
             m = work.tile([P, N], F32, name="m")
-            nc.scalar.activation(m[:], acc[:], ACT.Identity, bias=cols[:, ROW_FC2_B + k : ROW_FC2_B + k + 1])
+            for tokens in (slice(0, N),) if k < CB - 1 else (slice(0, N - LAST_TOKENS), slice(N - LAST_TOKENS, N)):
+                acc = bank(N)
+                for f in range(FB):
+                    weights = fc2w_sb[:, f, k * P : (k + 1) * P]
+                    nc.tensor.matmul(acc[:, tokens], weights, hid[f][:, tokens], start=(f == 0), stop=(f == FB - 1))
+                bias = cols[:, ROW_FC2_B + k : ROW_FC2_B + k + 1]
+                nc.scalar.activation(m[:, tokens], acc[:, tokens], ACT.Identity, bias=bias)
             nc.vector.tensor_tensor(window[k][:].indirect(offsets[:]), x_all[:, k, :], m[:], ALU.add)
             nc.sync.dma_start(out[k * P : (k + 1) * P, :], window[k][:])

@@ -61,12 +61,12 @@ def tile_splitgpt2_kernel(tc, base, x, ln_w, ln_b, fc_w, fc_b, fc2_w, fc2_b, off
         for k in range(CB):
             nc.sync.dma_start(window[k][:], base[k * P : (k + 1) * P, :])
 
-        idle_in = held.tile([P, P], F32, name="idle_in")
-        nc.vector.memset(idle_in[:], 1.0)
         ident = held.tile([P, P], F32, name="ident")
         make_identity(nc, ident[:])
         eps = held.tile([P, 1], F32, name="eps")
         nc.gpsimd.memset(eps[:], EPS)
+        table_early = held.tile([P, 1], F32, name="table_early")
+        nc.scalar.activation(table_early[:], eps[:], ACT.Abs_reciprocal_sqrt)
 
         def bank(columns):
             return banks.tile([P, columns], F32, name="bank")
@@ -75,7 +75,7 @@ def tile_splitgpt2_kernel(tc, base, x, ln_w, ln_b, fc_w, fc_b, fc2_w, fc2_b, off
 
         def idle_matmuls(count, moving):
             for i in range(count):
-                nc.tensor.matmul(idle_ps[:], idle_in[:], moving, start=True, stop=True)
+                nc.tensor.matmul(idle_ps[:], ident[:], moving, start=True, stop=True)
 
         HALF = CB // 2
         x_t = [[bank(HALF * P) for first_k in range(0, CB, HALF)] for t in range(TB)]
@@ -88,6 +88,7 @@ def tile_splitgpt2_kernel(tc, base, x, ln_w, ln_b, fc_w, fc_b, fc2_w, fc2_b, off
         nc.tensor.transpose(cols_ps[:], rows[:], ident[:])
         idle_matmuls(IDLE_UNTIL_NORMED, x_all[:, CB - 1, N - P :])
 
+        last_piece = held.tile([P, HALF * P], F32, name="last_piece")
         mean_var = [held.tile([P, 2], F32, name=f"mean_var{t}") for t in range(TB)]
         rstd = [held.tile([P, 1], F32, name=f"rstd{t}") for t in range(TB)]
         for t in range(TB):
@@ -95,15 +96,16 @@ def tile_splitgpt2_kernel(tc, base, x, ln_w, ln_b, fc_w, fc_b, fc2_w, fc2_b, off
             for i in range(2):
                 nc.vector.bn_stats(stats[:, i * 6 : (i + 1) * 6], x_t[t][i][:])
             nc.vector.bn_aggr(mean_var[t][:], stats[:])
+            if t == TB - 1:
+                nc.scalar.copy(last_piece[:], x_t[t][1][:])
             nc.scalar.activation(rstd[t][:], mean_var[t][:, 1:2], ACT.Abs_reciprocal_sqrt, bias=eps[:])
         normed = [held.tile([P, C], F32, name=f"normed{t}") for t in range(TB)]
         normed_t = [[bank(HALF * P) for first_k in range(0, CB, HALF)] for t in range(TB)]
         for t in range(TB):
             for first_k in range(0, CB, HALF):
                 half = slice(first_k * P, (first_k + HALF) * P)
-                nc.vector.tensor_scalar(
-                    normed[t][:, half], x_t[t][first_k // HALF][:], mean_var[t][:, 0:1], rstd[t][:], ALU.subtract, ALU.mult
-                )
+                source = last_piece if t == TB - 1 and first_k > 0 else x_t[t][first_k // HALF]
+                nc.vector.tensor_scalar(normed[t][:, half], source[:], mean_var[t][:, 0:1], rstd[t][:], ALU.subtract, ALU.mult)
                 for i in range(HALF):
                     k = first_k + i
                     nc.tensor.transpose(
@@ -111,7 +113,7 @@ def tile_splitgpt2_kernel(tc, base, x, ln_w, ln_b, fc_w, fc_b, fc2_w, fc2_b, off
                     )
 
         cols = held.tile([P, ROWS], F32, name="cols")
-        nc.vector.tensor_copy(cols[:], cols_ps[:, :ROWS])
+        nc.scalar.copy(cols[:], cols_ps[:, :ROWS])
 
         h = [held.tile([P, N], BF16, name=f"h{k}") for k in range(CB)]
         for t in range(TB):

@@ -88,24 +88,24 @@ def tile_splitgpt2_kernel(tc, base, x, ln_w, ln_b, fc_w, fc_b, fc2_w, fc2_b, off
         nc.tensor.transpose(cols_ps[:], rows[:], ident[:])
         idle_matmuls(IDLE_UNTIL_NORMED, x_all[:, CB - 1, N - P :])
 
-        last_piece = held.tile([P, HALF * P], F32, name="last_piece")
+        x_copy = [held.tile([P, C], F32, name=f"x_copy{t}") for t in range(TB)]
         mean_var = [held.tile([P, 2], F32, name=f"mean_var{t}") for t in range(TB)]
         rstd = [held.tile([P, 1], F32, name=f"rstd{t}") for t in range(TB)]
         for t in range(TB):
             stats = work.tile([P, 2 * 6], F32, name="stats")
             for i in range(2):
                 nc.vector.bn_stats(stats[:, i * 6 : (i + 1) * 6], x_t[t][i][:])
+                nc.scalar.copy(x_copy[t][:, i * HALF * P : (i + 1) * HALF * P], x_t[t][i][:])
             nc.vector.bn_aggr(mean_var[t][:], stats[:])
-            if t == TB - 1:
-                nc.scalar.copy(last_piece[:], x_t[t][1][:])
             nc.scalar.activation(rstd[t][:], mean_var[t][:, 1:2], ACT.Abs_reciprocal_sqrt, bias=eps[:])
         normed = [held.tile([P, C], F32, name=f"normed{t}") for t in range(TB)]
         normed_t = [[bank(HALF * P) for first_k in range(0, CB, HALF)] for t in range(TB)]
         for t in range(TB):
             for first_k in range(0, CB, HALF):
                 half = slice(first_k * P, (first_k + HALF) * P)
-                source = last_piece if t == TB - 1 and first_k > 0 else x_t[t][first_k // HALF]
-                nc.vector.tensor_scalar(normed[t][:, half], source[:], mean_var[t][:, 0:1], rstd[t][:], ALU.subtract, ALU.mult)
+                nc.vector.tensor_scalar(
+                    normed[t][:, half], x_copy[t][:, half], mean_var[t][:, 0:1], rstd[t][:], ALU.subtract, ALU.mult
+                )
                 for i in range(HALF):
                     k = first_k + i
                     nc.tensor.transpose(

import concourse.mybir as mybir
from concourse.masks import make_identity

F32, BF16, U16 = mybir.dt.float32, mybir.dt.bfloat16, mybir.dt.uint16
ACT = mybir.ActivationFunctionType
ALU = mybir.AluOpType

P = 128
C, F, S, N = 512, 2048, 1024, 256
CB, FB, TB = C // P, F // P, N // P
EPS = 1e-5
FLOPS = 2 * 2 * C * F * N

ROW_LN_W, ROW_LN_B, ROW_FC2_B, ROW_FC_B = 0, CB, 2 * CB, 3 * CB
ROWS = 3 * CB + FB

SIDE_BY_SIDE = 4

LAST_TOKENS = 64

FC_GROUP = 4

IDLE_UNTIL_NORMED = 3


def tile_splitgpt2_kernel(tc, base, x, ln_w, ln_b, fc_w, fc_b, fc2_w, fc2_b, offs, out):
    nc = tc.nc
    with (
        tc.tile_pool(name="held", bufs=1) as held,
        tc.tile_pool(name="work", bufs=2) as work,
        tc.psum_pool(name="banks", bufs=8) as banks,
    ):
        x_all = held.tile([P, CB, N], F32, name="x_all")
        x_view = x.rearrange("(k p) n -> p k n", p=P)
        for t in range(TB):
            for queue, first_k in ((nc.sync, 0), (nc.scalar, CB // 2)):
                queue.dma_start(
                    x_all[:, first_k : first_k + CB // 2, t * P : (t + 1) * P],
                    x_view[:, first_k : first_k + CB // 2, t * P : (t + 1) * P],
                )

        rows = held.tile([P, P], F32, name="rows")
        nc.gpsimd.memset(rows[:], 0.0)
        for vec, row, blocks in ((ln_w, ROW_LN_W, CB), (ln_b, ROW_LN_B, CB), (fc2_b, ROW_FC2_B, CB), (fc_b, ROW_FC_B, FB)):
            nc.sync.dma_start(rows[row : row + blocks, :], vec.rearrange("(b p) o -> b (p o)", p=P))

        fcw_sb = [held.tile([P, CB, FC_GROUP * P], BF16, name=f"fcw{g}") for g in range(FB // FC_GROUP)]
        fcw_view = fc_w.rearrange("(k p) f -> p k f", p=P)
        for g in range(FB // FC_GROUP):
            nc.sync.dma_start(fcw_sb[g][:], fcw_view[:, :, g * FC_GROUP * P : (g + 1) * FC_GROUP * P])

        def fcw_block(f, k):
            return fcw_sb[f // FC_GROUP][:, k, (f % FC_GROUP) * P : (f % FC_GROUP + 1) * P]
        fc2w_sb = held.tile([P, FB, C], BF16, name="fc2w")
        fc2w_view = fc2_w.rearrange("(fb p) c -> p fb c", p=P)
        for g in range(0, FB, 4):
            nc.sync.dma_start(fc2w_sb[:, g : g + 4, :], fc2w_view[:, g : g + 4, :])
        offsets = held.tile([P, N // 16], U16, name="offsets")
        nc.sync.dma_start(offsets[:], offs)
        window = [held.tile([P, S], F32, name=f"window{k}") for k in range(CB)]
        for k in range(CB):
            nc.sync.dma_start(window[k][:], base[k * P : (k + 1) * P, :])

        ident = held.tile([P, P], F32, name="ident")
        make_identity(nc, ident[:])
        eps = held.tile([P, 1], F32, name="eps")
        nc.gpsimd.memset(eps[:], EPS)
        table_early = held.tile([P, 1], F32, name="table_early")
        nc.scalar.activation(table_early[:], eps[:], ACT.Abs_reciprocal_sqrt)

        def bank(columns):
            return banks.tile([P, columns], F32, name="bank")

        idle_ps = bank(P)

        def idle_matmuls(count, moving):
            for i in range(count):
                nc.tensor.matmul(idle_ps[:], ident[:], moving, start=True, stop=True)

        HALF = CB // 2
        x_t = [[bank(HALF * P) for first_k in range(0, CB, HALF)] for t in range(TB)]
        cols_ps = bank(P)
        for t in range(TB):
            for k in range(CB):
                nc.tensor.transpose(
                    x_t[t][k // HALF][:, (k % HALF) * P : (k % HALF + 1) * P], x_all[:, k, t * P : (t + 1) * P], ident[:]
                )
        nc.tensor.transpose(cols_ps[:], rows[:], ident[:])
        idle_matmuls(IDLE_UNTIL_NORMED, x_all[:, CB - 1, N - P :])

        x_copy = [held.tile([P, C], F32, name=f"x_copy{t}") for t in range(TB)]
        mean_var = [held.tile([P, 2], F32, name=f"mean_var{t}") for t in range(TB)]
        rstd = [held.tile([P, 1], F32, name=f"rstd{t}") for t in range(TB)]
        for t in range(TB):
            stats = work.tile([P, 2 * 6], F32, name="stats")
            for i in range(2):
                nc.vector.bn_stats(stats[:, i * 6 : (i + 1) * 6], x_t[t][i][:])
                nc.scalar.copy(x_copy[t][:, i * HALF * P : (i + 1) * HALF * P], x_t[t][i][:])
            nc.vector.bn_aggr(mean_var[t][:], stats[:])
            nc.scalar.activation(rstd[t][:], mean_var[t][:, 1:2], ACT.Abs_reciprocal_sqrt, bias=eps[:])
        normed = [held.tile([P, C], F32, name=f"normed{t}") for t in range(TB)]
        normed_t = [[bank(HALF * P) for first_k in range(0, CB, HALF)] for t in range(TB)]
        for t in range(TB):
            for first_k in range(0, CB, HALF):
                half = slice(first_k * P, (first_k + HALF) * P)
                nc.vector.tensor_scalar(
                    normed[t][:, half], x_copy[t][:, half], mean_var[t][:, 0:1], rstd[t][:], ALU.subtract, ALU.mult
                )
                for i in range(HALF):
                    k = first_k + i
                    nc.tensor.transpose(
                        normed_t[t][first_k // HALF][:, i * P : (i + 1) * P], normed[t][:, k * P : (k + 1) * P], ident[:]
                    )

        cols = held.tile([P, ROWS], F32, name="cols")
        nc.scalar.copy(cols[:], cols_ps[:, :ROWS])

        h = [held.tile([P, N], BF16, name=f"h{k}") for k in range(CB)]
        for t in range(TB):
            for k in range(CB):
                gain, bias = cols[:, ROW_LN_W + k : ROW_LN_W + k + 1], cols[:, ROW_LN_B + k : ROW_LN_B + k + 1]
                turned = normed_t[t][k // HALF][:, (k % HALF) * P : (k % HALF + 1) * P]
                if t == 0:
                    nc.scalar.activation(h[k][:, t * P : (t + 1) * P], turned, ACT.Identity, bias=bias, scale=gain)
                else:
                    nc.vector.tensor_scalar(h[k][:, t * P : (t + 1) * P], turned, gain, bias, ALU.mult, ALU.add)

        hid = [held.tile([P, N], BF16, name=f"hid{f}") for f in range(FB)]

        def fc_matmul(acc, f, k):
            nc.tensor.matmul(acc[:], fcw_block(f, k), h[k][:], start=(k == 0), stop=(k == CB - 1))

        def gelu(acc, f):
            nc.scalar.activation(hid[f][:], acc[:], ACT.Gelu_apprx_tanh, bias=cols[:, ROW_FC_B + f : ROW_FC_B + f + 1])

        first = [bank(N) for f in range(SIDE_BY_SIDE)]
        for t in range(TB):
            tokens = slice(t * P, (t + 1) * P)
            for k in range(CB):
                for f in range(SIDE_BY_SIDE):
                    nc.tensor.matmul(first[f][:, tokens], fcw_block(f, k), h[k][:, tokens], start=(k == 0), stop=(k == CB - 1))
        for f in range(SIDE_BY_SIDE):
            gelu(first[f], f)
        for f in range(SIDE_BY_SIDE, FB):
            acc = bank(N)
            for k in range(CB):
                fc_matmul(acc, f, k)
            gelu(acc, f)

        for k in range(CB):
            m = work.tile([P, N], F32, name="m")
            for tokens in (slice(0, N),) if k < CB - 1 else (slice(0, N - LAST_TOKENS), slice(N - LAST_TOKENS, N)):
                acc = bank(N)
                for f in range(FB):
                    weights = fc2w_sb[:, f, k * P : (k + 1) * P]
                    nc.tensor.matmul(acc[:, tokens], weights, hid[f][:, tokens], start=(f == 0), stop=(f == FB - 1))
                bias = cols[:, ROW_FC2_B + k : ROW_FC2_B + k + 1]
                nc.scalar.activation(m[:, tokens], acc[:, tokens], ACT.Identity, bias=bias)
            nc.vector.tensor_tensor(window[k][:].indirect(offsets[:]), x_all[:, k, :], m[:], ALU.add)
            nc.sync.dma_start(out[k * P : (k + 1) * P, :], window[k][:])
